import numpy as np
import ml_dtypes


def mxq(x, axis, fmt="e4m3"):
    dtype, down = {"e4m3": (ml_dtypes.float8_e4m3fn, 7), "e5m2": (ml_dtypes.float8_e5m2, 14)}[fmt]
    v = np.moveaxis(np.asarray(x, np.float32).astype(ml_dtypes.bfloat16).astype(np.float64), axis, -1)
    blocks = v.reshape(v.shape[:-1] + (-1, 32))
    amax = np.abs(blocks).max(-1, keepdims=True)
    byte = np.maximum(np.where(amax > 0, np.frexp(amax)[1] - 1 + 127, 0) - down, 1)
    scale = np.exp2(byte - 127.0)
    codes = (blocks / scale).astype(np.float32).astype(dtype).astype(np.float64)
    return np.moveaxis((codes * scale).reshape(v.shape), -1, axis)


WIDE = False


def mx_kscale(k):
    if not WIDE:
        return np.ones(k)
    levels = np.array([10, -10, 5, -5, 0])
    a = np.random.permutation(np.resize(levels, k // 512 * 4)).reshape(k // 512, 4)
    idx = np.arange(k)
    return np.exp2(a[idx // 512, idx % 128 // 32])


BF16 = ml_dtypes.bfloat16


def bf(x):
    return np.asarray(x, np.float32).astype(BF16)


def f64(x):
    return np.asarray(x).astype(np.float64)


B, L, C, K, D_MODEL, H, D_LLM = 2, 64, 16, 100, 512, 32, 768
D_KEYS = D_MODEL // H
G = H * D_KEYS


def setup_inputs():
    s = mx_kscale(G).reshape(H, D_KEYS)
    return {
        "attn_ctx": bf(np.random.standard_normal((B, C, L, H, D_KEYS)) * 0.5 * s),
        "Wo": bf(np.random.standard_normal((C, H, D_KEYS, D_LLM)) * 2.0 / np.sqrt(G) / s[:, :, None]),
        "bo": bf(np.random.standard_normal((C, D_LLM)) * 0.5),
        "cluster_probs": bf(np.random.uniform(size=(B, L, C))),
    }


def reference(attn_ctx, Wo, bo, cluster_probs):
    o = f64(attn_ctx).reshape(B, C, L, G)
    w = f64(Wo).reshape(C, G, D_LLM)
    proj = mxq(o, 3, "e4m3") @ mxq(w, 1, "e4m3")
    aligned = proj.transpose(0, 2, 1, 3) + f64(bo)
    return (aligned * f64(cluster_probs)[:, :, :, None]).sum(-2)

@@ -1,0 +1,199 @@
+from contextlib import ExitStack
+
+import concourse.masks as masks
+import concourse.mybir as mybir
+
+BF16 = mybir.dt.bfloat16
+F32 = mybir.dt.float32
+U32 = mybir.dt.uint32
+U8 = mybir.dt.uint8
+FP8X4 = mybir.dt.float8_e4m3fn_x4
+MULT = mybir.AluOpType.mult
+ADD = mybir.AluOpType.add
+
+P = 128
+PACK = 4
+HALVES = 2
+B, C, L, G, E = 2, 16, 64, 512, 768
+TOKENS = B * L
+PAIRS = C // 2
+assert TOKENS == P and G == P * PACK
+
+N_WIDE = 512
+N_NARROW = E - N_WIDE
+WIDE = slice(0, N_WIDE)
+NARROW = slice(N_WIDE, E)
+RUN = 4
+
+FLOPS = 2 * TOKENS * C * G * E
+
+
+def tile_model_pa_kernel(tc, attn_ctx, Wo, bo, cluster_probs, out):
+    nc = tc.nc
+    with ExitStack() as ctx:
+        consts = ctx.enter_context(tc.tile_pool(name="consts", bufs=1))
+        a_in = ctx.enter_context(tc.tile_pool(name="a_in", bufs=PAIRS))
+        w_in = ctx.enter_context(tc.tile_pool(name="w_in", bufs=C))
+        work = ctx.enter_context(tc.tile_pool(name="work", bufs=3))
+        psum = ctx.enter_context(tc.psum_pool(name="psum", bufs=2))
+        ctx.enter_context(tc.manual_schedule())
+
+        a_rows = attn_ctx.rearrange("b c l h d -> b (c l) (h d)")
+        a_raw = []
+        w_raw = []
+        for pair in range(PAIRS):
+            a_tile = a_in.tile([P, B * G], BF16, name="a_raw")
+            nc.sync.dma_start(
+                out=a_tile[:].rearrange("r (b k) -> r b k", b=B),
+                in_=a_rows[:, pair * P : (pair + 1) * P, :].rearrange("b r k -> r b k"),
+            )
+            a_raw.append(a_tile)
+            for c in (2 * pair, 2 * pair + 1):
+                w_tile = w_in.tile([P, PACK, E], BF16, name="w_raw")
+                nc.sync.dma_start(
+                    out=w_tile[:],
+                    in_=Wo[c].rearrange("h d e -> (h d) e").rearrange("(p t) e -> p t e", t=PACK),
+                )
+                w_raw.append(w_tile)
+
+        probs_bf16 = consts.tile([P, C], BF16)
+        nc.scalar.dma_start(out=probs_bf16[:], in_=cluster_probs.rearrange("b l c -> (b l) c"))
+        bo_rows = consts.tile([P, E], BF16)
+        nc.vector.memset(bo_rows[:], 0.0)
+        nc.scalar.dma_start(out=bo_rows[0:C, :], in_=bo[:, :])
+        identity = consts.tile([P, P], F32)
+        masks.make_identity(nc, identity[:])
+        probs = consts.tile([P, P], F32)
+        nc.vector.memset(probs[:], 0.0)
+        nc.vector.tensor_copy(out=probs[:, 0:C], in_=probs_bf16[:])
+
+        a_codes = {}
+        a_grouped = {}
+        w_grouped = {}
+        w_codes = {}
+        projected = {}
+        fused = consts.tile([P, E], F32)
+
+        def transpose_a(pair):
+            words = a_raw[pair][:].bitcast(F32).rearrange("r (b p u) -> r b u p", b=B, u=HALVES)
+            turned = psum.tile([P, B, HALVES, 2, L], F32, name="a_turned")
+            for b in range(B):
+                for u in range(HALVES):
+                    nc.tensor.transpose(
+                        turned[:, b, u, :, :].rearrange("p c l -> p (c l)"), words[:, b, u, :], identity[:]
+                    )
+            grouped = work.tile([P, 2 * TOKENS * PACK], BF16, name="a_grouped", align_bytes=64)
+            grouped_words = grouped[:].bitcast(F32)
+            for c_in_pair in range(2):
+                nc.scalar.copy(
+                    out=grouped_words[
+                        :, c_in_pair * TOKENS * HALVES : (c_in_pair + 1) * TOKENS * HALVES
+                    ].rearrange("p (b l u) -> p b l u", b=B, u=HALVES),
+                    in_=turned[:, :, :, c_in_pair, :].rearrange("p b u l -> p b l u"),
+                )
+            a_grouped[pair] = grouped
+
+        def quantise_a(pair):
+            codes = work.tile([P, 2 * TOKENS], U32, name="a_codes", align_bytes=64)
+            scales = work.tile([P, 2 * TOKENS], U8, name="a_scales", align_bytes=64)
+            nc.vector.quantize_mx(out=codes[:].bitcast(FP8X4), scales=scales[:], in_=a_grouped[pair][:])
+            a_codes[pair] = (codes, scales)
+
+        def regroup(copy, grouped, raw_columns):
+            copy(
+                out=grouped[:].rearrange("p (n i) t -> p n t i", i=RUN),
+                in_=raw_columns.rearrange("p t (n i) -> p n t i", i=RUN),
+            )
+
+        def regroup_w(c):
+            wide = work.tile([P, N_WIDE, PACK], BF16, name="w_grouped_wide", align_bytes=64)
+            narrow = work.tile([P, N_NARROW, PACK], BF16, name="w_grouped_narrow", align_bytes=64)
+            regroup(nc.scalar.copy, wide, w_raw[c][:, :, WIDE])
+            regroup(nc.vector.tensor_copy, narrow, w_raw[c][:, :, NARROW])
+            w_grouped[c] = (wide, narrow)
+
+        def quantise_w(c):
+            wide, narrow = w_grouped[c]
+            wide_codes = work.tile([P, N_WIDE], U32, name="w_codes_wide", align_bytes=64)
+            wide_scales = work.tile([P, N_WIDE], U8, name="w_scales_wide", align_bytes=64)
+            narrow_codes = work.tile([P, N_NARROW], U32, name="w_codes_narrow", align_bytes=64)
+            narrow_scales = work.tile([P, N_NARROW], U8, name="w_scales_narrow", align_bytes=64)
+            nc.vector.quantize_mx(
+                out=wide_codes[:].bitcast(FP8X4),
+                scales=wide_scales[:],
+                in_=wide[:].rearrange("p n t -> p (n t)"),
+            )
+            nc.vector.quantize_mx(
+                out=narrow_codes[:].bitcast(FP8X4),
+                scales=narrow_scales[:],
+                in_=narrow[:].rearrange("p n t -> p (n t)"),
+            )
+            w_codes[c] = (wide_codes, wide_scales, narrow_codes, narrow_scales)
+
+        def project(c):
+            tokens_codes, tokens_scales = a_codes[c // 2]
+            tokens = slice((c % 2) * TOKENS, (c % 2 + 1) * TOKENS)
+            wide_codes, wide_scales, narrow_codes, narrow_scales = w_codes[c]
+            wide = psum.tile([P, N_WIDE], F32, name="projected_wide")
+            narrow = psum.tile([P, N_NARROW], F32, name="projected_narrow")
+            nc.tensor.matmul_mx(
+                out=wide[:],
+                lhsT=tokens_codes[:, tokens].bitcast(FP8X4),
+                lhsT_scale=tokens_scales[:, tokens],
+                rhs=wide_codes[:].bitcast(FP8X4),
+                rhs_scale=wide_scales[:],
+                start=True,
+                stop=True,
+            )
+            nc.tensor.matmul_mx(
+                out=narrow[:],
+                lhsT=tokens_codes[:, tokens].bitcast(FP8X4),
+                lhsT_scale=tokens_scales[:, tokens],
+                rhs=narrow_codes[:].bitcast(FP8X4),
+                rhs_scale=narrow_scales[:],
+                start=True,
+                stop=True,
+            )
+            projected[c] = (wide, narrow)
+
+        def mix(c):
+            wide, narrow = projected[c]
+            for part, columns in ((wide, WIDE), (narrow, NARROW)):
+                nc.vector.scalar_tensor_tensor(
+                    out=fused[:, columns],
+                    in0=part[:],
+                    scalar=probs[:, c : c + 1],
+                    in1=fused[:, columns],
+                    op0=MULT,
+                    op1=ADD,
+                )
+
+        transpose_a(0)
+        quantise_a(0)
+        probs_turned = psum.tile([P, P], F32, name="probs_turned", bufs=1)
+        nc.tensor.transpose(probs_turned[:], probs[:], identity[:])
+        probs_t = consts.tile([P, P], BF16)
+        nc.vector.tensor_copy(out=probs_t[:], in_=probs_turned[:])
+        bias_wide = psum.tile([P, N_WIDE], F32, name="projected_wide")
+        bias_narrow = psum.tile([P, N_NARROW], F32, name="projected_narrow")
+        nc.tensor.matmul(out=bias_wide[:], lhsT=probs_t[:], rhs=bo_rows[:, WIDE], start=True, stop=True)
+        nc.tensor.matmul(out=bias_narrow[:], lhsT=probs_t[:], rhs=bo_rows[:, NARROW], start=True, stop=True)
+
+        regroup_w(0)
+        nc.scalar.copy(out=fused[:, WIDE], in_=bias_wide[:])
+        nc.scalar.copy(out=fused[:, NARROW], in_=bias_narrow[:])
+
+        for c in range(1, C + 1):
+            quantise_w(c - 1)
+            if c < C:
+                regroup_w(c)
+            if c % 2 == 0 and c < C:
+                quantise_a(c // 2)
+            project(c - 1)
+            if c % 2 == 1 and c + 1 < C:
+                transpose_a((c + 1) // 2)
+            mix(c - 1)
+
+        out_rows = out.rearrange("b l e -> (b l) e")
+        nc.sync.dma_start(out=out_rows[:, WIDE], in_=fused[:, WIDE])
+        nc.sync.dma_start(out=out_rows[:, NARROW], in_=fused[:, NARROW])

@@ -23,6 +23,9 @@ N_WIDE = 512
 N_NARROW = E - N_WIDE
 WIDE = slice(0, N_WIDE)
 NARROW = slice(N_WIDE, E)
+N_SCALAR = 512
+SCALAR_COLUMNS = slice(0, N_SCALAR)
+VECTOR_COLUMNS = slice(N_SCALAR, E)
 RUN = 4
 
 FLOPS = 2 * TOKENS * C * G * E
@@ -38,6 +41,10 @@ def tile_model_pa_kernel(tc, attn_ctx, Wo, bo, cluster_probs, out):
         psum = ctx.enter_context(tc.psum_pool(name="psum", bufs=2))
         ctx.enter_context(tc.manual_schedule())
 
+        probs_bf16 = consts.tile([P, C], BF16)
+        nc.sync.dma_start(out=probs_bf16[:], in_=cluster_probs.rearrange("b l c -> (b l) c"))
+        bo_rows = consts.tile([P, E], BF16)
+        nc.vector.memset(bo_rows[:], 0.0)
         a_rows = attn_ctx.rearrange("b c l h d -> b (c l) (h d)")
         a_raw = []
         w_raw = []
@@ -55,12 +62,9 @@ def tile_model_pa_kernel(tc, attn_ctx, Wo, bo, cluster_probs, out):
                     in_=Wo[c].rearrange("h d e -> (h d) e").rearrange("(p t) e -> p t e", t=PACK),
                 )
                 w_raw.append(w_tile)
+                if c == 0:
+                    nc.sync.dma_start(out=bo_rows[0:C, :], in_=bo[:, :])
 
-        probs_bf16 = consts.tile([P, C], BF16)
-        nc.scalar.dma_start(out=probs_bf16[:], in_=cluster_probs.rearrange("b l c -> (b l) c"))
-        bo_rows = consts.tile([P, E], BF16)
-        nc.vector.memset(bo_rows[:], 0.0)
-        nc.scalar.dma_start(out=bo_rows[0:C, :], in_=bo[:, :])
         identity = consts.tile([P, P], F32)
         masks.make_identity(nc, identity[:])
         probs = consts.tile([P, P], F32)
@@ -68,13 +72,14 @@ def tile_model_pa_kernel(tc, attn_ctx, Wo, bo, cluster_probs, out):
         nc.vector.tensor_copy(out=probs[:, 0:C], in_=probs_bf16[:])
 
         a_codes = {}
+        a_turned = {}
         a_grouped = {}
         w_grouped = {}
         w_codes = {}
         projected = {}
         fused = consts.tile([P, E], F32)
 
-        def transpose_a(pair):
+        def turn_a(pair):
             words = a_raw[pair][:].bitcast(F32).rearrange("r (b p u) -> r b u p", b=B, u=HALVES)
             turned = psum.tile([P, B, HALVES, 2, L], F32, name="a_turned")
             for b in range(B):
@@ -82,6 +87,10 @@ def tile_model_pa_kernel(tc, attn_ctx, Wo, bo, cluster_probs, out):
                     nc.tensor.transpose(
                         turned[:, b, u, :, :].rearrange("p c l -> p (c l)"), words[:, b, u, :], identity[:]
                     )
+            a_turned[pair] = turned
+
+        def regroup_a(pair):
+            turned = a_turned[pair]
             grouped = work.tile([P, 2 * TOKENS * PACK], BF16, name="a_grouped", align_bytes=64)
             grouped_words = grouped[:].bitcast(F32)
             for c_in_pair in range(2):
@@ -101,19 +110,18 @@ def tile_model_pa_kernel(tc, attn_ctx, Wo, bo, cluster_probs, out):
 
         def regroup(copy, grouped, raw_columns):
             copy(
-                out=grouped[:].rearrange("p (n i) t -> p n t i", i=RUN),
+                out=grouped.rearrange("p (n i) t -> p n t i", i=RUN),
                 in_=raw_columns.rearrange("p t (n i) -> p n t i", i=RUN),
             )
 
         def regroup_w(c):
-            wide = work.tile([P, N_WIDE, PACK], BF16, name="w_grouped_wide", align_bytes=64)
-            narrow = work.tile([P, N_NARROW, PACK], BF16, name="w_grouped_narrow", align_bytes=64)
-            regroup(nc.scalar.copy, wide, w_raw[c][:, :, WIDE])
-            regroup(nc.vector.tensor_copy, narrow, w_raw[c][:, :, NARROW])
-            w_grouped[c] = (wide, narrow)
+            grouped = work.tile([P, E, PACK], BF16, name="w_grouped", align_bytes=64)
+            regroup(nc.scalar.copy, grouped[:, SCALAR_COLUMNS, :], w_raw[c][:, :, SCALAR_COLUMNS])
+            regroup(nc.vector.tensor_copy, grouped[:, VECTOR_COLUMNS, :], w_raw[c][:, :, VECTOR_COLUMNS])
+            w_grouped[c] = grouped
 
         def quantise_w(c):
-            wide, narrow = w_grouped[c]
+            grouped = w_grouped[c]
             wide_codes = work.tile([P, N_WIDE], U32, name="w_codes_wide", align_bytes=64)
             wide_scales = work.tile([P, N_WIDE], U8, name="w_scales_wide", align_bytes=64)
             narrow_codes = work.tile([P, N_NARROW], U32, name="w_codes_narrow", align_bytes=64)
@@ -121,12 +129,12 @@ def tile_model_pa_kernel(tc, attn_ctx, Wo, bo, cluster_probs, out):
             nc.vector.quantize_mx(
                 out=wide_codes[:].bitcast(FP8X4),
                 scales=wide_scales[:],
-                in_=wide[:].rearrange("p n t -> p (n t)"),
+                in_=grouped[:, WIDE, :].rearrange("p n t -> p (n t)"),
             )
             nc.vector.quantize_mx(
                 out=narrow_codes[:].bitcast(FP8X4),
                 scales=narrow_scales[:],
-                in_=narrow[:].rearrange("p n t -> p (n t)"),
+                in_=grouped[:, NARROW, :].rearrange("p n t -> p (n t)"),
             )
             w_codes[c] = (wide_codes, wide_scales, narrow_codes, narrow_scales)
 
@@ -168,8 +176,8 @@ def tile_model_pa_kernel(tc, attn_ctx, Wo, bo, cluster_probs, out):
                     op1=ADD,
                 )
 
-        transpose_a(0)
-        quantise_a(0)
+        turn_a(0)
+        regroup_a(0)
         probs_turned = psum.tile([P, P], F32, name="probs_turned", bufs=1)
         nc.tensor.transpose(probs_turned[:], probs[:], identity[:])
         probs_t = consts.tile([P, P], BF16)
@@ -180,19 +188,26 @@ def tile_model_pa_kernel(tc, attn_ctx, Wo, bo, cluster_probs, out):
         nc.tensor.matmul(out=bias_narrow[:], lhsT=probs_t[:], rhs=bo_rows[:, NARROW], start=True, stop=True)
 
         regroup_w(0)
-        nc.scalar.copy(out=fused[:, WIDE], in_=bias_wide[:])
-        nc.scalar.copy(out=fused[:, NARROW], in_=bias_narrow[:])
+        quantise_a(0)
+        nc.vector.tensor_copy(out=fused[:, WIDE], in_=bias_wide[:])
+        nc.vector.tensor_copy(out=fused[:, NARROW], in_=bias_narrow[:])
 
-        for c in range(1, C + 1):
-            quantise_w(c - 1)
+        for c in range(1, C + 2):
+            next_pair_starts = c % 2 == 1 and c + 1 < C
+            if next_pair_starts:
+                turn_a((c + 1) // 2)
+            if c <= C:
+                quantise_w(c - 1)
+            if c >= 2:
+                mix(c - 2)
             if c < C:
                 regroup_w(c)
+            if next_pair_starts:
+                regroup_a((c + 1) // 2)
             if c % 2 == 0 and c < C:
                 quantise_a(c // 2)
-            project(c - 1)
-            if c % 2 == 1 and c + 1 < C:
-                transpose_a((c + 1) // 2)
-            mix(c - 1)
+            if c <= C:
+                project(c - 1)
 
         out_rows = out.rearrange("b l e -> (b l) e")
         nc.sync.dma_start(out=out_rows[:, WIDE], in_=fused[:, WIDE])

@@ -23,9 +23,11 @@ N_WIDE = 512
 N_NARROW = E - N_WIDE
 WIDE = slice(0, N_WIDE)
 NARROW = slice(N_WIDE, E)
-N_SCALAR = 512
+N_SCALAR = 464
+N_GPSIMD = 128
 SCALAR_COLUMNS = slice(0, N_SCALAR)
-VECTOR_COLUMNS = slice(N_SCALAR, E)
+VECTOR_COLUMNS = slice(N_SCALAR, E - N_GPSIMD)
+GPSIMD_COLUMNS = slice(E - N_GPSIMD, E)
 RUN = 4
 
 FLOPS = 2 * TOKENS * C * G * E
@@ -114,11 +116,17 @@ def tile_model_pa_kernel(tc, attn_ctx, Wo, bo, cluster_probs, out):
                 in_=raw_columns.rearrange("p t (n i) -> p n t i", i=RUN),
             )
 
-        def regroup_w(c):
-            grouped = work.tile([P, E, PACK], BF16, name="w_grouped", align_bytes=64)
-            regroup(nc.scalar.copy, grouped[:, SCALAR_COLUMNS, :], w_raw[c][:, :, SCALAR_COLUMNS])
+        def gpsimd_copy(out, in_):
+            nc.gpsimd.tensor_scalar(out=out, in0=in_, scalar1=1.0, scalar2=0.0, op0=MULT, op1=ADD)
+
+        def start_regrouping_w(c):
+            grouped = work.tile([P, E, PACK], BF16, name="w_grouped", bufs=2, align_bytes=64)
+            regroup(gpsimd_copy, grouped[:, GPSIMD_COLUMNS, :], w_raw[c][:, :, GPSIMD_COLUMNS])
             regroup(nc.vector.tensor_copy, grouped[:, VECTOR_COLUMNS, :], w_raw[c][:, :, VECTOR_COLUMNS])
             w_grouped[c] = grouped
+
+        def finish_regrouping_w(c):
+            regroup(nc.scalar.copy, w_grouped[c][:, SCALAR_COLUMNS, :], w_raw[c][:, :, SCALAR_COLUMNS])
 
         def quantise_w(c):
             grouped = w_grouped[c]
@@ -187,10 +195,12 @@ def tile_model_pa_kernel(tc, attn_ctx, Wo, bo, cluster_probs, out):
         nc.tensor.matmul(out=bias_wide[:], lhsT=probs_t[:], rhs=bo_rows[:, WIDE], start=True, stop=True)
         nc.tensor.matmul(out=bias_narrow[:], lhsT=probs_t[:], rhs=bo_rows[:, NARROW], start=True, stop=True)
 
-        regroup_w(0)
+        start_regrouping_w(0)
+        finish_regrouping_w(0)
         quantise_a(0)
         nc.vector.tensor_copy(out=fused[:, WIDE], in_=bias_wide[:])
         nc.vector.tensor_copy(out=fused[:, NARROW], in_=bias_narrow[:])
+        start_regrouping_w(1)
 
         for c in range(1, C + 2):
             next_pair_starts = c % 2 == 1 and c + 1 < C
@@ -200,8 +210,10 @@ def tile_model_pa_kernel(tc, attn_ctx, Wo, bo, cluster_probs, out):
                 quantise_w(c - 1)
             if c >= 2:
                 mix(c - 2)
+            if c + 1 < C:
+                start_regrouping_w(c + 1)
             if c < C:
-                regroup_w(c)
+                finish_regrouping_w(c)
             if next_pair_starts:
                 regroup_a((c + 1) // 2)
             if c % 2 == 0 and c < C:

@@ -24,7 +24,7 @@ N_NARROW = E - N_WIDE
 WIDE = slice(0, N_WIDE)
 NARROW = slice(N_WIDE, E)
 N_SCALAR = 464
-N_GPSIMD = 128
+N_GPSIMD = 144
 SCALAR_COLUMNS = slice(0, N_SCALAR)
 VECTOR_COLUMNS = slice(N_SCALAR, E - N_GPSIMD)
 GPSIMD_COLUMNS = slice(E - N_GPSIMD, E)
@@ -116,16 +116,22 @@ def tile_model_pa_kernel(tc, attn_ctx, Wo, bo, cluster_probs, out):
                 in_=raw_columns.rearrange("p t (n i) -> p n t i", i=RUN),
             )
 
-        def gpsimd_copy(out, in_):
-            nc.gpsimd.tensor_scalar(out=out, in0=in_, scalar1=1.0, scalar2=0.0, op0=MULT, op1=ADD)
-
-        def start_regrouping_w(c):
+        def gpsimd_regroups_w(c):
             grouped = work.tile([P, E, PACK], BF16, name="w_grouped", bufs=2, align_bytes=64)
-            regroup(gpsimd_copy, grouped[:, GPSIMD_COLUMNS, :], w_raw[c][:, :, GPSIMD_COLUMNS])
-            regroup(nc.vector.tensor_copy, grouped[:, VECTOR_COLUMNS, :], w_raw[c][:, :, VECTOR_COLUMNS])
+            nc.gpsimd.tensor_scalar(
+                out=grouped[:, GPSIMD_COLUMNS, :],
+                in0=w_raw[c][:, :, GPSIMD_COLUMNS].rearrange("p t n -> p n t"),
+                scalar1=1.0,
+                scalar2=0.0,
+                op0=MULT,
+                op1=ADD,
+            )
             w_grouped[c] = grouped
 
-        def finish_regrouping_w(c):
+        def vector_regroups_w(c):
+            regroup(nc.vector.tensor_copy, w_grouped[c][:, VECTOR_COLUMNS, :], w_raw[c][:, :, VECTOR_COLUMNS])
+
+        def scalar_regroups_w(c):
             regroup(nc.scalar.copy, w_grouped[c][:, SCALAR_COLUMNS, :], w_raw[c][:, :, SCALAR_COLUMNS])
 
         def quantise_w(c):
@@ -195,12 +201,13 @@ def tile_model_pa_kernel(tc, attn_ctx, Wo, bo, cluster_probs, out):
         nc.tensor.matmul(out=bias_wide[:], lhsT=probs_t[:], rhs=bo_rows[:, WIDE], start=True, stop=True)
         nc.tensor.matmul(out=bias_narrow[:], lhsT=probs_t[:], rhs=bo_rows[:, NARROW], start=True, stop=True)
 
-        start_regrouping_w(0)
-        finish_regrouping_w(0)
+        gpsimd_regroups_w(0)
+        gpsimd_regroups_w(1)
+        vector_regroups_w(0)
+        scalar_regroups_w(0)
         quantise_a(0)
         nc.vector.tensor_copy(out=fused[:, WIDE], in_=bias_wide[:])
         nc.vector.tensor_copy(out=fused[:, NARROW], in_=bias_narrow[:])
-        start_regrouping_w(1)
 
         for c in range(1, C + 2):
             next_pair_starts = c % 2 == 1 and c + 1 < C
@@ -208,16 +215,18 @@ def tile_model_pa_kernel(tc, attn_ctx, Wo, bo, cluster_probs, out):
                 turn_a((c + 1) // 2)
             if c <= C:
                 quantise_w(c - 1)
-            if c >= 2:
-                mix(c - 2)
             if c + 1 < C:
-                start_regrouping_w(c + 1)
+                gpsimd_regroups_w(c + 1)
             if c < C:
-                finish_regrouping_w(c)
-            if next_pair_starts:
-                regroup_a((c + 1) // 2)
+                vector_regroups_w(c)
             if c % 2 == 0 and c < C:
                 quantise_a(c // 2)
+            if c >= 2:
+                mix(c - 2)
+            if c < C:
+                scalar_regroups_w(c)
+            if next_pair_starts:
+                regroup_a((c + 1) // 2)
             if c <= C:
                 project(c - 1)
 

@@ -77,7 +77,8 @@ def tile_model_pa_kernel(tc, attn_ctx, Wo, bo, cluster_probs, out):
         a_turned = {}
         a_grouped = {}
         w_grouped = {}
-        w_codes = {}
+        w_codes_wide = {}
+        w_codes_narrow = {}
         projected = {}
         fused = consts.tile([P, E], F32)
 
@@ -134,28 +135,31 @@ def tile_model_pa_kernel(tc, attn_ctx, Wo, bo, cluster_probs, out):
         def scalar_regroups_w(c):
             regroup(nc.scalar.copy, w_grouped[c][:, SCALAR_COLUMNS, :], w_raw[c][:, :, SCALAR_COLUMNS])
 
-        def quantise_w(c):
-            grouped = w_grouped[c]
+        def quantise_w_wide(c):
             wide_codes = work.tile([P, N_WIDE], U32, name="w_codes_wide", align_bytes=64)
             wide_scales = work.tile([P, N_WIDE], U8, name="w_scales_wide", align_bytes=64)
-            narrow_codes = work.tile([P, N_NARROW], U32, name="w_codes_narrow", align_bytes=64)
-            narrow_scales = work.tile([P, N_NARROW], U8, name="w_scales_narrow", align_bytes=64)
             nc.vector.quantize_mx(
                 out=wide_codes[:].bitcast(FP8X4),
                 scales=wide_scales[:],
-                in_=grouped[:, WIDE, :].rearrange("p n t -> p (n t)"),
+                in_=w_grouped[c][:, WIDE, :].rearrange("p n t -> p (n t)"),
             )
+            w_codes_wide[c] = (wide_codes, wide_scales)
+
+        def quantise_w_narrow(c):
+            narrow_codes = work.tile([P, N_NARROW], U32, name="w_codes_narrow", align_bytes=64)
+            narrow_scales = work.tile([P, N_NARROW], U8, name="w_scales_narrow", align_bytes=64)
             nc.vector.quantize_mx(
                 out=narrow_codes[:].bitcast(FP8X4),
                 scales=narrow_scales[:],
-                in_=grouped[:, NARROW, :].rearrange("p n t -> p (n t)"),
+                in_=w_grouped[c][:, NARROW, :].rearrange("p n t -> p (n t)"),
             )
-            w_codes[c] = (wide_codes, wide_scales, narrow_codes, narrow_scales)
+            w_codes_narrow[c] = (narrow_codes, narrow_scales)
 
         def project(c):
             tokens_codes, tokens_scales = a_codes[c // 2]
             tokens = slice((c % 2) * TOKENS, (c % 2 + 1) * TOKENS)
-            wide_codes, wide_scales, narrow_codes, narrow_scales = w_codes[c]
+            wide_codes, wide_scales = w_codes_wide[c]
+            narrow_codes, narrow_scales = w_codes_narrow[c]
             wide = psum.tile([P, N_WIDE], F32, name="projected_wide")
             narrow = psum.tile([P, N_NARROW], F32, name="projected_narrow")
             nc.tensor.matmul_mx(
@@ -214,13 +218,15 @@ def tile_model_pa_kernel(tc, attn_ctx, Wo, bo, cluster_probs, out):
             if next_pair_starts:
                 turn_a((c + 1) // 2)
             if c <= C:
-                quantise_w(c - 1)
+                quantise_w_wide(c - 1)
+            if c % 2 == 0 and c < C:
+                quantise_a(c // 2)
+            if c <= C:
+                quantise_w_narrow(c - 1)
             if c + 1 < C:
                 gpsimd_regroups_w(c + 1)
             if c < C:
                 vector_regroups_w(c)
-            if c % 2 == 0 and c < C:
-                quantise_a(c // 2)
             if c >= 2:
                 mix(c - 2)
             if c < C:

@@ -23,11 +23,10 @@ N_WIDE = 512
 N_NARROW = E - N_WIDE
 WIDE = slice(0, N_WIDE)
 NARROW = slice(N_WIDE, E)
-N_SCALAR = 464
 N_GPSIMD = 144
-SCALAR_COLUMNS = slice(0, N_SCALAR)
-VECTOR_COLUMNS = slice(N_SCALAR, E - N_GPSIMD)
-GPSIMD_COLUMNS = slice(E - N_GPSIMD, E)
+N_VECTOR = 160
+VECTOR_SHARE = {0: 496, 1: 480, 2: 352, C - 1: 0}
+GPSIMD_SHARE = {0: 0, 1: 0}
 RUN = 4
 
 FLOPS = 2 * TOKENS * C * G * E
@@ -44,34 +43,41 @@ def tile_model_pa_kernel(tc, attn_ctx, Wo, bo, cluster_probs, out):
         ctx.enter_context(tc.manual_schedule())
 
         probs_bf16 = consts.tile([P, C], BF16)
-        nc.sync.dma_start(out=probs_bf16[:], in_=cluster_probs.rearrange("b l c -> (b l) c"))
         bo_rows = consts.tile([P, E], BF16)
         nc.vector.memset(bo_rows[:], 0.0)
         a_rows = attn_ctx.rearrange("b c l h d -> b (c l) (h d)")
         a_raw = []
         w_raw = []
-        for pair in range(PAIRS):
+        def load_a(pair):
             a_tile = a_in.tile([P, B * G], BF16, name="a_raw")
             nc.sync.dma_start(
                 out=a_tile[:].rearrange("r (b k) -> r b k", b=B),
                 in_=a_rows[:, pair * P : (pair + 1) * P, :].rearrange("b r k -> r b k"),
             )
             a_raw.append(a_tile)
-            for c in (2 * pair, 2 * pair + 1):
-                w_tile = w_in.tile([P, PACK, E], BF16, name="w_raw")
-                nc.sync.dma_start(
-                    out=w_tile[:],
-                    in_=Wo[c].rearrange("h d e -> (h d) e").rearrange("(p t) e -> p t e", t=PACK),
-                )
-                w_raw.append(w_tile)
-                if c == 0:
-                    nc.sync.dma_start(out=bo_rows[0:C, :], in_=bo[:, :])
+
+        def load_w(c):
+            w_tile = w_in.tile([P, PACK, E], BF16, name="w_raw")
+            nc.sync.dma_start(
+                out=w_tile[:],
+                in_=Wo[c].rearrange("h d e -> (h d) e").rearrange("(p t) e -> p t e", t=PACK),
+            )
+            w_raw.append(w_tile)
+
+        load_w(0)
+        load_a(0)
+        nc.sync.dma_start(out=probs_bf16[:], in_=cluster_probs.rearrange("b l c -> (b l) c"))
+        nc.sync.dma_start(out=bo_rows[0:C, :], in_=bo[:, :])
+        load_w(1)
+        for pair in range(1, PAIRS):
+            load_a(pair)
+            load_w(2 * pair)
+            load_w(2 * pair + 1)
 
         identity = consts.tile([P, P], F32)
         masks.make_identity(nc, identity[:])
         probs = consts.tile([P, P], F32)
         nc.vector.memset(probs[:], 0.0)
-        nc.vector.tensor_copy(out=probs[:, 0:C], in_=probs_bf16[:])
 
         a_codes = {}
         a_turned = {}
@@ -79,7 +85,8 @@ def tile_model_pa_kernel(tc, attn_ctx, Wo, bo, cluster_probs, out):
         w_grouped = {}
         w_codes_wide = {}
         w_codes_narrow = {}
-        projected = {}
+        projected_wide = {}
+        projected_narrow = {}
         fused = consts.tile([P, E], F32)
 
         def turn_a(pair):
@@ -119,21 +126,29 @@ def tile_model_pa_kernel(tc, attn_ctx, Wo, bo, cluster_probs, out):
 
         def gpsimd_regroups_w(c):
             grouped = work.tile([P, E, PACK], BF16, name="w_grouped", bufs=2, align_bytes=64)
-            nc.gpsimd.tensor_scalar(
-                out=grouped[:, GPSIMD_COLUMNS, :],
-                in0=w_raw[c][:, :, GPSIMD_COLUMNS].rearrange("p t n -> p n t"),
-                scalar1=1.0,
-                scalar2=0.0,
-                op0=MULT,
-                op1=ADD,
-            )
             w_grouped[c] = grouped
+            columns = slice(E - GPSIMD_SHARE.get(c, N_GPSIMD), E)
+            if columns.start < E:
+                nc.gpsimd.tensor_scalar(
+                    out=grouped[:, columns, :],
+                    in0=w_raw[c][:, :, columns].rearrange("p t n -> p n t"),
+                    scalar1=1.0,
+                    scalar2=0.0,
+                    op0=MULT,
+                    op1=ADD,
+                )
 
         def vector_regroups_w(c):
-            regroup(nc.vector.tensor_copy, w_grouped[c][:, VECTOR_COLUMNS, :], w_raw[c][:, :, VECTOR_COLUMNS])
+            stop = E - GPSIMD_SHARE.get(c, N_GPSIMD)
+            columns = slice(stop - VECTOR_SHARE.get(c, N_VECTOR), stop)
+            if columns.start < stop:
+                regroup(nc.vector.tensor_copy, w_grouped[c][:, columns, :], w_raw[c][:, :, columns])
 
         def scalar_regroups_w(c):
-            regroup(nc.scalar.copy, w_grouped[c][:, SCALAR_COLUMNS, :], w_raw[c][:, :, SCALAR_COLUMNS])
+            stop = E - GPSIMD_SHARE.get(c, N_GPSIMD) - VECTOR_SHARE.get(c, N_VECTOR)
+            for columns in (slice(0, min(stop, N_WIDE)), slice(N_WIDE, stop)):
+                if columns.start < columns.stop:
+                    regroup(nc.scalar.copy, w_grouped[c][:, columns, :], w_raw[c][:, :, columns])
 
         def quantise_w_wide(c):
             wide_codes = work.tile([P, N_WIDE], U32, name="w_codes_wide", align_bytes=64)
@@ -155,36 +170,32 @@ def tile_model_pa_kernel(tc, attn_ctx, Wo, bo, cluster_probs, out):
             )
             w_codes_narrow[c] = (narrow_codes, narrow_scales)
 
-        def project(c):
+        def project_part(c, codes_and_scales, part):
             tokens_codes, tokens_scales = a_codes[c // 2]
             tokens = slice((c % 2) * TOKENS, (c % 2 + 1) * TOKENS)
-            wide_codes, wide_scales = w_codes_wide[c]
-            narrow_codes, narrow_scales = w_codes_narrow[c]
+            codes, scales = codes_and_scales
+            nc.tensor.matmul_mx(
+                out=part[:],
+                lhsT=tokens_codes[:, tokens].bitcast(FP8X4),
+                lhsT_scale=tokens_scales[:, tokens],
+                rhs=codes[:].bitcast(FP8X4),
+                rhs_scale=scales[:],
+                start=True,
+                stop=True,
+            )
+
+        def project_wide(c):
             wide = psum.tile([P, N_WIDE], F32, name="projected_wide")
+            project_part(c, w_codes_wide[c], wide)
+            projected_wide[c] = wide
+
+        def project_narrow(c):
             narrow = psum.tile([P, N_NARROW], F32, name="projected_narrow")
-            nc.tensor.matmul_mx(
-                out=wide[:],
-                lhsT=tokens_codes[:, tokens].bitcast(FP8X4),
-                lhsT_scale=tokens_scales[:, tokens],
-                rhs=wide_codes[:].bitcast(FP8X4),
-                rhs_scale=wide_scales[:],
-                start=True,
-                stop=True,
-            )
-            nc.tensor.matmul_mx(
-                out=narrow[:],
-                lhsT=tokens_codes[:, tokens].bitcast(FP8X4),
-                lhsT_scale=tokens_scales[:, tokens],
-                rhs=narrow_codes[:].bitcast(FP8X4),
-                rhs_scale=narrow_scales[:],
-                start=True,
-                stop=True,
-            )
-            projected[c] = (wide, narrow)
+            project_part(c, w_codes_narrow[c], narrow)
+            projected_narrow[c] = narrow
 
         def mix(c):
-            wide, narrow = projected[c]
-            for part, columns in ((wide, WIDE), (narrow, NARROW)):
+            for part, columns in ((projected_wide[c], WIDE), (projected_narrow[c], NARROW)):
                 nc.vector.scalar_tensor_tensor(
                     out=fused[:, columns],
                     in0=part[:],
@@ -194,47 +205,69 @@ def tile_model_pa_kernel(tc, attn_ctx, Wo, bo, cluster_probs, out):
                     op1=ADD,
                 )
 
+        gpsimd_regroups_w(0)
+        vector_regroups_w(0)
+        scalar_regroups_w(0)
         turn_a(0)
-        regroup_a(0)
+        nc.vector.tensor_copy(out=probs[:, 0:C], in_=probs_bf16[:])
         probs_turned = psum.tile([P, P], F32, name="probs_turned", bufs=1)
         nc.tensor.transpose(probs_turned[:], probs[:], identity[:])
+        regroup_a(0)
+
+        quantise_w_wide(0)
+        quantise_w_narrow(0)
         probs_t = consts.tile([P, P], BF16)
         nc.vector.tensor_copy(out=probs_t[:], in_=probs_turned[:])
         bias_wide = psum.tile([P, N_WIDE], F32, name="projected_wide")
         bias_narrow = psum.tile([P, N_NARROW], F32, name="projected_narrow")
         nc.tensor.matmul(out=bias_wide[:], lhsT=probs_t[:], rhs=bo_rows[:, WIDE], start=True, stop=True)
         nc.tensor.matmul(out=bias_narrow[:], lhsT=probs_t[:], rhs=bo_rows[:, NARROW], start=True, stop=True)
-
-        gpsimd_regroups_w(0)
-        gpsimd_regroups_w(1)
-        vector_regroups_w(0)
-        scalar_regroups_w(0)
         quantise_a(0)
-        nc.vector.tensor_copy(out=fused[:, WIDE], in_=bias_wide[:])
-        nc.vector.tensor_copy(out=fused[:, NARROW], in_=bias_narrow[:])
+        gpsimd_regroups_w(1)
+        vector_regroups_w(1)
+        scalar_regroups_w(1)
+        project_wide(0)
+        project_narrow(0)
+        turn_a(1)
+        nc.scalar.copy(out=fused[:, WIDE], in_=bias_wide[:])
+        nc.scalar.copy(out=fused[:, NARROW], in_=bias_narrow[:])
+        regroup_a(1)
 
-        for c in range(1, C + 2):
+        quantise_w_wide(1)
+        quantise_w_narrow(1)
+        gpsimd_regroups_w(2)
+        vector_regroups_w(2)
+        quantise_a(1)
+        gpsimd_regroups_w(3)
+        mix(0)
+        scalar_regroups_w(2)
+        project_wide(1)
+        project_narrow(1)
+
+        for c in range(3, C):
             next_pair_starts = c % 2 == 1 and c + 1 < C
             if next_pair_starts:
                 turn_a((c + 1) // 2)
-            if c <= C:
-                quantise_w_wide(c - 1)
-            if c % 2 == 0 and c < C:
-                quantise_a(c // 2)
-            if c <= C:
-                quantise_w_narrow(c - 1)
+            quantise_w_wide(c - 1)
+            quantise_w_narrow(c - 1)
             if c + 1 < C:
                 gpsimd_regroups_w(c + 1)
-            if c < C:
-                vector_regroups_w(c)
-            if c >= 2:
-                mix(c - 2)
-            if c < C:
-                scalar_regroups_w(c)
+            vector_regroups_w(c)
+            if c % 2 == 0:
+                quantise_a(c // 2)
+            mix(c - 2)
+            scalar_regroups_w(c)
             if next_pair_starts:
                 regroup_a((c + 1) // 2)
-            if c <= C:
-                project(c - 1)
+            project_wide(c - 1)
+            project_narrow(c - 1)
+
+        quantise_w_wide(C - 1)
+        project_wide(C - 1)
+        mix(C - 2)
+        quantise_w_narrow(C - 1)
+        project_narrow(C - 1)
+        mix(C - 1)
 
         out_rows = out.rearrange("b l e -> (b l) e")
         nc.sync.dma_start(out=out_rows[:, WIDE], in_=fused[:, WIDE])

@@ -27,6 +27,7 @@ N_GPSIMD = 144
 N_VECTOR = 160
 VECTOR_SHARE = {0: 496, 1: 480, 2: 352, C - 1: 0}
 GPSIMD_SHARE = {0: 0, 1: 0}
+N_TENSOR = 64
 RUN = 4
 
 FLOPS = 2 * TOKENS * C * G * E
@@ -76,6 +77,8 @@ def tile_model_pa_kernel(tc, attn_ctx, Wo, bo, cluster_probs, out):
 
         identity = consts.tile([P, P], F32)
         masks.make_identity(nc, identity[:])
+        identity_bf16 = consts.tile([P, P], BF16)
+        masks.make_identity(nc, identity_bf16[:])
         probs = consts.tile([P, P], F32)
         nc.vector.memset(probs[:], 0.0)
 
@@ -83,6 +86,7 @@ def tile_model_pa_kernel(tc, attn_ctx, Wo, bo, cluster_probs, out):
         a_turned = {}
         a_grouped = {}
         w_grouped = {}
+        w_routed = {}
         w_codes_wide = {}
         w_codes_narrow = {}
         projected_wide = {}
@@ -144,8 +148,24 @@ def tile_model_pa_kernel(tc, attn_ctx, Wo, bo, cluster_probs, out):
             if columns.start < stop:
                 regroup(nc.vector.tensor_copy, w_grouped[c][:, columns, :], w_raw[c][:, :, columns])
 
-        def scalar_regroups_w(c):
+        def tensor_regroups_w(c):
             stop = E - GPSIMD_SHARE.get(c, N_GPSIMD) - VECTOR_SHARE.get(c, N_VECTOR)
+            routed = psum.tile([P, N_TENSOR, PACK], BF16, name="routed")
+            nc.tensor.matmul(
+                out=routed[:],
+                lhsT=identity_bf16[:],
+                rhs=w_raw[c][:, :, stop - N_TENSOR : stop].rearrange("p t n -> p n t"),
+                start=True,
+                stop=True,
+            )
+            w_routed[c] = routed
+
+        def scalar_takes_routed(c):
+            stop = E - GPSIMD_SHARE.get(c, N_GPSIMD) - VECTOR_SHARE.get(c, N_VECTOR)
+            nc.scalar.copy(out=w_grouped[c][:, stop - N_TENSOR : stop, :], in_=w_routed[c][:])
+
+        def scalar_regroups_w(c):
+            stop = E - GPSIMD_SHARE.get(c, N_GPSIMD) - VECTOR_SHARE.get(c, N_VECTOR) - N_TENSOR
             for columns in (slice(0, min(stop, N_WIDE)), slice(N_WIDE, stop)):
                 if columns.start < columns.stop:
                     regroup(nc.scalar.copy, w_grouped[c][:, columns, :], w_raw[c][:, :, columns])
@@ -207,10 +227,12 @@ def tile_model_pa_kernel(tc, attn_ctx, Wo, bo, cluster_probs, out):
 
         gpsimd_regroups_w(0)
         vector_regroups_w(0)
+        tensor_regroups_w(0)
         scalar_regroups_w(0)
+        scalar_takes_routed(0)
         turn_a(0)
         nc.vector.tensor_copy(out=probs[:, 0:C], in_=probs_bf16[:])
-        probs_turned = psum.tile([P, P], F32, name="probs_turned", bufs=1)
+        probs_turned = psum.tile([P, P], F32, name="routed")
         nc.tensor.transpose(probs_turned[:], probs[:], identity[:])
         regroup_a(0)
 
@@ -225,7 +247,9 @@ def tile_model_pa_kernel(tc, attn_ctx, Wo, bo, cluster_probs, out):
         quantise_a(0)
         gpsimd_regroups_w(1)
         vector_regroups_w(1)
+        tensor_regroups_w(1)
         scalar_regroups_w(1)
+        scalar_takes_routed(1)
         project_wide(0)
         project_narrow(0)
         turn_a(1)
@@ -240,7 +264,9 @@ def tile_model_pa_kernel(tc, attn_ctx, Wo, bo, cluster_probs, out):
         quantise_a(1)
         gpsimd_regroups_w(3)
         mix(0)
+        tensor_regroups_w(2)
         scalar_regroups_w(2)
+        scalar_takes_routed(2)
         project_wide(1)
         project_narrow(1)
 
@@ -248,6 +274,7 @@ def tile_model_pa_kernel(tc, attn_ctx, Wo, bo, cluster_probs, out):
             next_pair_starts = c % 2 == 1 and c + 1 < C
             if next_pair_starts:
                 turn_a((c + 1) // 2)
+            tensor_regroups_w(c)
             quantise_w_wide(c - 1)
             quantise_w_narrow(c - 1)
             if c + 1 < C:
@@ -257,6 +284,7 @@ def tile_model_pa_kernel(tc, attn_ctx, Wo, bo, cluster_probs, out):
                 quantise_a(c // 2)
             mix(c - 2)
             scalar_regroups_w(c)
+            scalar_takes_routed(c)
             if next_pair_starts:
                 regroup_a((c + 1) // 2)
             project_wide(c - 1)

@@ -29,6 +29,7 @@ VECTOR_SHARE = {0: 496, 1: 480, 2: 352, C - 1: 0}
 GPSIMD_SHARE = {0: 0, 1: 0}
 N_TENSOR = 64
 RUN = 4
+RUN_SCALAR = 8
 
 FLOPS = 2 * TOKENS * C * G * E
 
@@ -122,10 +123,10 @@ def tile_model_pa_kernel(tc, attn_ctx, Wo, bo, cluster_probs, out):
             nc.vector.quantize_mx(out=codes[:].bitcast(FP8X4), scales=scales[:], in_=a_grouped[pair][:])
             a_codes[pair] = (codes, scales)
 
-        def regroup(copy, grouped, raw_columns):
+        def regroup(copy, grouped, raw_columns, run=RUN):
             copy(
-                out=grouped.rearrange("p (n i) t -> p n t i", i=RUN),
-                in_=raw_columns.rearrange("p t (n i) -> p n t i", i=RUN),
+                out=grouped.rearrange("p (n i) t -> p n t i", i=run),
+                in_=raw_columns.rearrange("p t (n i) -> p n t i", i=run),
             )
 
         def gpsimd_regroups_w(c):
@@ -168,7 +169,7 @@ def tile_model_pa_kernel(tc, attn_ctx, Wo, bo, cluster_probs, out):
             stop = E - GPSIMD_SHARE.get(c, N_GPSIMD) - VECTOR_SHARE.get(c, N_VECTOR) - N_TENSOR
             for columns in (slice(0, min(stop, N_WIDE)), slice(N_WIDE, stop)):
                 if columns.start < columns.stop:
-                    regroup(nc.scalar.copy, w_grouped[c][:, columns, :], w_raw[c][:, :, columns])
+                    regroup(nc.scalar.copy, w_grouped[c][:, columns, :], w_raw[c][:, :, columns], run=RUN_SCALAR)
 
         def quantise_w_wide(c):
             wide_codes = work.tile([P, N_WIDE], U32, name="w_codes_wide", align_bytes=64)

@@ -28,7 +28,7 @@ N_VECTOR = 160
 VECTOR_SHARE = {0: 496, 1: 480, 2: 352, C - 1: 0}
 GPSIMD_SHARE = {0: 0, 1: 0}
 N_TENSOR = 64
-RUN = 4
+RUN = 8
 RUN_SCALAR = 8
 
 FLOPS = 2 * TOKENS * C * G * E

@@ -24,7 +24,7 @@ N_NARROW = E - N_WIDE
 WIDE = slice(0, N_WIDE)
 NARROW = slice(N_WIDE, E)
 N_GPSIMD = 144
-N_VECTOR = 160
+N_VECTOR = 144
 VECTOR_SHARE = {0: 496, 1: 480, 2: 352, C - 1: 0}
 GPSIMD_SHARE = {0: 0, 1: 0}
 N_TENSOR = 64

@@ -23,13 +23,14 @@ N_WIDE = 512
 N_NARROW = E - N_WIDE
 WIDE = slice(0, N_WIDE)
 NARROW = slice(N_WIDE, E)
-N_GPSIMD = 144
+N_GPSIMD = 160
 N_VECTOR = 144
 VECTOR_SHARE = {0: 496, 1: 480, 2: 352, C - 1: 0}
 GPSIMD_SHARE = {0: 0, 1: 0}
 N_TENSOR = 64
 RUN = 8
 RUN_SCALAR = 8
+RUN_GPSIMD = 4
 
 FLOPS = 2 * TOKENS * C * G * E
 
@@ -135,8 +136,8 @@ def tile_model_pa_kernel(tc, attn_ctx, Wo, bo, cluster_probs, out):
             columns = slice(E - GPSIMD_SHARE.get(c, N_GPSIMD), E)
             if columns.start < E:
                 nc.gpsimd.tensor_scalar(
-                    out=grouped[:, columns, :],
-                    in0=w_raw[c][:, :, columns].rearrange("p t n -> p n t"),
+                    out=grouped[:, columns, :].rearrange("p (n i) t -> p n t i", i=RUN_GPSIMD),
+                    in0=w_raw[c][:, :, columns].rearrange("p t (n i) -> p n t i", i=RUN_GPSIMD),
                     scalar1=1.0,
                     scalar2=0.0,
                     op0=MULT,

@@ -23,8 +23,12 @@ N_WIDE = 512
 N_NARROW = E - N_WIDE
 WIDE = slice(0, N_WIDE)
 NARROW = slice(N_WIDE, E)
+FIRST = slice(0, N_NARROW)
+SECOND = slice(N_NARROW, N_WIDE)
+COLUMNS = {"wide": WIDE, "narrow": NARROW, "first": FIRST, "second": SECOND}
+SIZE = {N_WIDE: "wide", N_NARROW: "narrow"}
 N_GPSIMD = 160
-N_VECTOR = 144
+N_VECTOR = 128
 VECTOR_SHARE = {0: 496, 1: 480, 2: 352, C - 1: 0}
 GPSIMD_SHARE = {0: 0, 1: 0}
 N_TENSOR = 64
@@ -45,7 +49,8 @@ def tile_model_pa_kernel(tc, attn_ctx, Wo, bo, cluster_probs, out):
         psum = ctx.enter_context(tc.psum_pool(name="psum", bufs=2))
         ctx.enter_context(tc.manual_schedule())
 
-        probs_bf16 = consts.tile([P, C], BF16)
+        probs_bf16 = consts.tile([P, P], BF16)
+        nc.vector.memset(probs_bf16[:, C:], 0.0)
         bo_rows = consts.tile([P, E], BF16)
         nc.vector.memset(bo_rows[:], 0.0)
         a_rows = attn_ctx.rearrange("b c l h d -> b (c l) (h d)")
@@ -69,7 +74,7 @@ def tile_model_pa_kernel(tc, attn_ctx, Wo, bo, cluster_probs, out):
 
         load_w(0)
         load_a(0)
-        nc.sync.dma_start(out=probs_bf16[:], in_=cluster_probs.rearrange("b l c -> (b l) c"))
+        nc.sync.dma_start(out=probs_bf16[:, 0:C], in_=cluster_probs.rearrange("b l c -> (b l) c"))
         nc.sync.dma_start(out=bo_rows[0:C, :], in_=bo[:, :])
         load_w(1)
         for pair in range(1, PAIRS):
@@ -81,18 +86,15 @@ def tile_model_pa_kernel(tc, attn_ctx, Wo, bo, cluster_probs, out):
         masks.make_identity(nc, identity[:])
         identity_bf16 = consts.tile([P, P], BF16)
         masks.make_identity(nc, identity_bf16[:])
-        probs = consts.tile([P, P], F32)
-        nc.vector.memset(probs[:], 0.0)
+        probs = consts.tile([P, C], F32)
 
         a_codes = {}
         a_turned = {}
         a_grouped = {}
         w_grouped = {}
         w_routed = {}
-        w_codes_wide = {}
-        w_codes_narrow = {}
-        projected_wide = {}
-        projected_narrow = {}
+        w_codes = {}
+        projected = {}
         fused = consts.tile([P, E], F32)
 
         def turn_a(pair):
@@ -168,36 +170,37 @@ def tile_model_pa_kernel(tc, attn_ctx, Wo, bo, cluster_probs, out):
 
         def scalar_regroups_w(c):
             stop = E - GPSIMD_SHARE.get(c, N_GPSIMD) - VECTOR_SHARE.get(c, N_VECTOR) - N_TENSOR
-            for columns in (slice(0, min(stop, N_WIDE)), slice(N_WIDE, stop)):
-                if columns.start < columns.stop:
-                    regroup(nc.scalar.copy, w_grouped[c][:, columns, :], w_raw[c][:, :, columns], run=RUN_SCALAR)
+            for columns in (slice(N_WIDE, stop), FIRST, SECOND) if c == C - 1 else (slice(0, stop),):
+                regroup(nc.scalar.copy, w_grouped[c][:, columns, :], w_raw[c][:, :, columns], run=RUN_SCALAR)
+                if columns.stop == stop:
+                    scalar_takes_routed(c)
+
+        def quantise_w(c, part):
+            columns = COLUMNS[part]
+            width = columns.stop - columns.start
+            codes = work.tile([P, width], U32, name="w_codes_" + SIZE[width], align_bytes=64)
+            scales = work.tile([P, width], U8, name="w_scales_" + SIZE[width], align_bytes=64)
+            nc.vector.quantize_mx(
+                out=codes[:].bitcast(FP8X4),
+                scales=scales[:],
+                in_=w_grouped[c][:, columns, :].rearrange("p n t -> p (n t)"),
+            )
+            w_codes[c, part] = (codes, scales)
 
         def quantise_w_wide(c):
-            wide_codes = work.tile([P, N_WIDE], U32, name="w_codes_wide", align_bytes=64)
-            wide_scales = work.tile([P, N_WIDE], U8, name="w_scales_wide", align_bytes=64)
-            nc.vector.quantize_mx(
-                out=wide_codes[:].bitcast(FP8X4),
-                scales=wide_scales[:],
-                in_=w_grouped[c][:, WIDE, :].rearrange("p n t -> p (n t)"),
-            )
-            w_codes_wide[c] = (wide_codes, wide_scales)
+            quantise_w(c, "wide")
 
         def quantise_w_narrow(c):
-            narrow_codes = work.tile([P, N_NARROW], U32, name="w_codes_narrow", align_bytes=64)
-            narrow_scales = work.tile([P, N_NARROW], U8, name="w_scales_narrow", align_bytes=64)
-            nc.vector.quantize_mx(
-                out=narrow_codes[:].bitcast(FP8X4),
-                scales=narrow_scales[:],
-                in_=w_grouped[c][:, NARROW, :].rearrange("p n t -> p (n t)"),
-            )
-            w_codes_narrow[c] = (narrow_codes, narrow_scales)
+            quantise_w(c, "narrow")
 
-        def project_part(c, codes_and_scales, part):
+        def project(c, part):
             tokens_codes, tokens_scales = a_codes[c // 2]
             tokens = slice((c % 2) * TOKENS, (c % 2 + 1) * TOKENS)
-            codes, scales = codes_and_scales
+            codes, scales = w_codes[c, part]
+            width = COLUMNS[part].stop - COLUMNS[part].start
+            out_tile = psum.tile([P, width], F32, name="projected_" + SIZE[width])
             nc.tensor.matmul_mx(
-                out=part[:],
+                out=out_tile[:],
                 lhsT=tokens_codes[:, tokens].bitcast(FP8X4),
                 lhsT_scale=tokens_scales[:, tokens],
                 rhs=codes[:].bitcast(FP8X4),
@@ -205,43 +208,43 @@ def tile_model_pa_kernel(tc, attn_ctx, Wo, bo, cluster_probs, out):
                 start=True,
                 stop=True,
             )
+            projected[c, part] = out_tile
 
-        def project_wide(c):
-            wide = psum.tile([P, N_WIDE], F32, name="projected_wide")
-            project_part(c, w_codes_wide[c], wide)
-            projected_wide[c] = wide
+        def mix(c, part):
+            columns = COLUMNS[part]
+            nc.vector.scalar_tensor_tensor(
+                out=fused[:, columns],
+                in0=projected[c, part][:],
+                scalar=probs[:, c : c + 1],
+                in1=fused[:, columns],
+                op0=MULT,
+                op1=ADD,
+            )
 
         def project_narrow(c):
-            narrow = psum.tile([P, N_NARROW], F32, name="projected_narrow")
-            project_part(c, w_codes_narrow[c], narrow)
-            projected_narrow[c] = narrow
+            project(c, "narrow")
 
-        def mix(c):
-            for part, columns in ((projected_wide[c], WIDE), (projected_narrow[c], NARROW)):
-                nc.vector.scalar_tensor_tensor(
-                    out=fused[:, columns],
-                    in0=part[:],
-                    scalar=probs[:, c : c + 1],
-                    in1=fused[:, columns],
-                    op0=MULT,
-                    op1=ADD,
-                )
+        def project_wide(c):
+            project(c, "wide")
+
+        def mix_both(c):
+            mix(c, "wide")
+            mix(c, "narrow")
 
         gpsimd_regroups_w(0)
         vector_regroups_w(0)
         tensor_regroups_w(0)
         scalar_regroups_w(0)
-        scalar_takes_routed(0)
         turn_a(0)
-        nc.vector.tensor_copy(out=probs[:, 0:C], in_=probs_bf16[:])
-        probs_turned = psum.tile([P, P], F32, name="routed")
-        nc.tensor.transpose(probs_turned[:], probs[:], identity[:])
+        nc.vector.tensor_copy(out=probs[:], in_=probs_bf16[:, 0:C])
+        probs_turned = psum.tile([P, P], BF16, name="routed")
+        nc.tensor.transpose(probs_turned[:], probs_bf16[:], identity_bf16[:])
         regroup_a(0)
+        probs_t = consts.tile([P, P], BF16)
+        nc.scalar.copy(out=probs_t[:], in_=probs_turned[:])
 
         quantise_w_wide(0)
         quantise_w_narrow(0)
-        probs_t = consts.tile([P, P], BF16)
-        nc.vector.tensor_copy(out=probs_t[:], in_=probs_turned[:])
         bias_wide = psum.tile([P, N_WIDE], F32, name="projected_wide")
         bias_narrow = psum.tile([P, N_NARROW], F32, name="projected_narrow")
         nc.tensor.matmul(out=bias_wide[:], lhsT=probs_t[:], rhs=bo_rows[:, WIDE], start=True, stop=True)
@@ -251,7 +254,6 @@ def tile_model_pa_kernel(tc, attn_ctx, Wo, bo, cluster_probs, out):
         vector_regroups_w(1)
         tensor_regroups_w(1)
         scalar_regroups_w(1)
-        scalar_takes_routed(1)
         project_wide(0)
         project_narrow(0)
         turn_a(1)
@@ -265,10 +267,9 @@ def tile_model_pa_kernel(tc, attn_ctx, Wo, bo, cluster_probs, out):
         vector_regroups_w(2)
         quantise_a(1)
         gpsimd_regroups_w(3)
-        mix(0)
+        mix_both(0)
         tensor_regroups_w(2)
         scalar_regroups_w(2)
-        scalar_takes_routed(2)
         project_wide(1)
         project_narrow(1)
 
@@ -284,21 +285,24 @@ def tile_model_pa_kernel(tc, attn_ctx, Wo, bo, cluster_probs, out):
             vector_regroups_w(c)
             if c % 2 == 0:
                 quantise_a(c // 2)
-            mix(c - 2)
+            mix_both(c - 2)
             scalar_regroups_w(c)
-            scalar_takes_routed(c)
             if next_pair_starts:
                 regroup_a((c + 1) // 2)
             project_wide(c - 1)
             project_narrow(c - 1)
 
-        quantise_w_wide(C - 1)
-        project_wide(C - 1)
-        mix(C - 2)
         quantise_w_narrow(C - 1)
         project_narrow(C - 1)
-        mix(C - 1)
+        mix_both(C - 2)
+        quantise_w(C - 1, "first")
+        project(C - 1, "first")
+        mix(C - 1, "narrow")
+        quantise_w(C - 1, "second")
+        project(C - 1, "second")
+        mix(C - 1, "first")
+        mix(C - 1, "second")
 
         out_rows = out.rearrange("b l e -> (b l) e")
-        nc.sync.dma_start(out=out_rows[:, WIDE], in_=fused[:, WIDE])
-        nc.sync.dma_start(out=out_rows[:, NARROW], in_=fused[:, NARROW])
+        for columns in (NARROW, FIRST, SECOND):
+            nc.sync.dma_start(out=out_rows[:, columns], in_=fused[:, columns])

@@ -166,7 +166,10 @@ def tile_model_pa_kernel(tc, attn_ctx, Wo, bo, cluster_probs, out):
 
         def scalar_takes_routed(c):
             stop = E - GPSIMD_SHARE.get(c, N_GPSIMD) - VECTOR_SHARE.get(c, N_VECTOR)
-            nc.scalar.copy(out=w_grouped[c][:, stop - N_TENSOR : stop, :], in_=w_routed[c][:])
+            nc.scalar.copy(
+                out=w_grouped[c][:, stop - N_TENSOR : stop, :].rearrange("p n t -> p (n t)").bitcast(F32),
+                in_=w_routed[c][:].rearrange("p n t -> p (n t)").bitcast(F32),
+            )
 
         def scalar_regroups_w(c):
             stop = E - GPSIMD_SHARE.get(c, N_GPSIMD) - VECTOR_SHARE.get(c, N_VECTOR) - N_TENSOR
@@ -245,15 +248,15 @@ def tile_model_pa_kernel(tc, attn_ctx, Wo, bo, cluster_probs, out):
 
         quantise_w_wide(0)
         quantise_w_narrow(0)
-        bias_wide = psum.tile([P, N_WIDE], F32, name="projected_wide")
-        bias_narrow = psum.tile([P, N_NARROW], F32, name="projected_narrow")
-        nc.tensor.matmul(out=bias_wide[:], lhsT=probs_t[:], rhs=bo_rows[:, WIDE], start=True, stop=True)
-        nc.tensor.matmul(out=bias_narrow[:], lhsT=probs_t[:], rhs=bo_rows[:, NARROW], start=True, stop=True)
         quantise_a(0)
         gpsimd_regroups_w(1)
         vector_regroups_w(1)
         tensor_regroups_w(1)
         scalar_regroups_w(1)
+        bias_wide = psum.tile([P, N_WIDE], F32, name="projected_wide")
+        bias_narrow = psum.tile([P, N_NARROW], F32, name="projected_narrow")
+        nc.tensor.matmul(out=bias_wide[:], lhsT=probs_t[:], rhs=bo_rows[:, WIDE], start=True, stop=True)
+        nc.tensor.matmul(out=bias_narrow[:], lhsT=probs_t[:], rhs=bo_rows[:, NARROW], start=True, stop=True)
         project_wide(0)
         project_narrow(0)
         turn_a(1)

@@ -27,9 +27,12 @@ FIRST = slice(0, N_NARROW)
 SECOND = slice(N_NARROW, N_WIDE)
 COLUMNS = {"wide": WIDE, "narrow": NARROW, "first": FIRST, "second": SECOND}
 SIZE = {N_WIDE: "wide", N_NARROW: "narrow"}
+BANKS = {"wide": "wide", "narrow": "narrow", "first": "wide", "second": "narrow"}
 N_GPSIMD = 160
-N_VECTOR = 128
-VECTOR_SHARE = {0: 496, 1: 480, 2: 352, C - 1: 0}
+N_VECTOR_ODD = 128
+N_VECTOR_EVEN = 112
+VECTOR_AT_THE_ENDS = {0: 528, 1: 480, 2: 400, C - 1: 0}
+VECTOR_SHARE = {c: VECTOR_AT_THE_ENDS.get(c, N_VECTOR_ODD if c % 2 == 1 else N_VECTOR_EVEN) for c in range(C)}
 GPSIMD_SHARE = {0: 0, 1: 0}
 N_TENSOR = 64
 RUN = 8
@@ -111,13 +114,10 @@ def tile_model_pa_kernel(tc, attn_ctx, Wo, bo, cluster_probs, out):
             turned = a_turned[pair]
             grouped = work.tile([P, 2 * TOKENS * PACK], BF16, name="a_grouped", align_bytes=64)
             grouped_words = grouped[:].bitcast(F32)
-            for c_in_pair in range(2):
-                nc.scalar.copy(
-                    out=grouped_words[
-                        :, c_in_pair * TOKENS * HALVES : (c_in_pair + 1) * TOKENS * HALVES
-                    ].rearrange("p (b l u) -> p b l u", b=B, u=HALVES),
-                    in_=turned[:, :, :, c_in_pair, :].rearrange("p b u l -> p b l u"),
-                )
+            nc.scalar.copy(
+                out=grouped_words.rearrange("p (c b l u) -> p b c l u", c=2, b=B, u=HALVES),
+                in_=turned[:].rearrange("p b u c l -> p b c l u"),
+            )
             a_grouped[pair] = grouped
 
         def quantise_a(pair):
@@ -148,12 +148,12 @@ def tile_model_pa_kernel(tc, attn_ctx, Wo, bo, cluster_probs, out):
 
         def vector_regroups_w(c):
             stop = E - GPSIMD_SHARE.get(c, N_GPSIMD)
-            columns = slice(stop - VECTOR_SHARE.get(c, N_VECTOR), stop)
+            columns = slice(stop - VECTOR_SHARE[c], stop)
             if columns.start < stop:
                 regroup(nc.vector.tensor_copy, w_grouped[c][:, columns, :], w_raw[c][:, :, columns])
 
         def tensor_regroups_w(c):
-            stop = E - GPSIMD_SHARE.get(c, N_GPSIMD) - VECTOR_SHARE.get(c, N_VECTOR)
+            stop = E - GPSIMD_SHARE.get(c, N_GPSIMD) - VECTOR_SHARE[c]
             routed = psum.tile([P, N_TENSOR, PACK], BF16, name="routed")
             nc.tensor.matmul(
                 out=routed[:],
@@ -165,14 +165,14 @@ def tile_model_pa_kernel(tc, attn_ctx, Wo, bo, cluster_probs, out):
             w_routed[c] = routed
 
         def scalar_takes_routed(c):
-            stop = E - GPSIMD_SHARE.get(c, N_GPSIMD) - VECTOR_SHARE.get(c, N_VECTOR)
+            stop = E - GPSIMD_SHARE.get(c, N_GPSIMD) - VECTOR_SHARE[c]
             nc.scalar.copy(
                 out=w_grouped[c][:, stop - N_TENSOR : stop, :].rearrange("p n t -> p (n t)").bitcast(F32),
                 in_=w_routed[c][:].rearrange("p n t -> p (n t)").bitcast(F32),
             )
 
         def scalar_regroups_w(c):
-            stop = E - GPSIMD_SHARE.get(c, N_GPSIMD) - VECTOR_SHARE.get(c, N_VECTOR) - N_TENSOR
+            stop = E - GPSIMD_SHARE.get(c, N_GPSIMD) - VECTOR_SHARE[c] - N_TENSOR
             for columns in (slice(N_WIDE, stop), FIRST, SECOND) if c == C - 1 else (slice(0, stop),):
                 regroup(nc.scalar.copy, w_grouped[c][:, columns, :], w_raw[c][:, :, columns], run=RUN_SCALAR)
                 if columns.stop == stop:
@@ -201,7 +201,7 @@ def tile_model_pa_kernel(tc, attn_ctx, Wo, bo, cluster_probs, out):
             tokens = slice((c % 2) * TOKENS, (c % 2 + 1) * TOKENS)
             codes, scales = w_codes[c, part]
             width = COLUMNS[part].stop - COLUMNS[part].start
-            out_tile = psum.tile([P, width], F32, name="projected_" + SIZE[width])
+            out_tile = psum.tile([P, width], F32, name="projected_" + BANKS[part])
             nc.tensor.matmul_mx(
                 out=out_tile[:],
                 lhsT=tokens_codes[:, tokens].bitcast(FP8X4),
@@ -257,9 +257,9 @@ def tile_model_pa_kernel(tc, attn_ctx, Wo, bo, cluster_probs, out):
         bias_narrow = psum.tile([P, N_NARROW], F32, name="projected_narrow")
         nc.tensor.matmul(out=bias_wide[:], lhsT=probs_t[:], rhs=bo_rows[:, WIDE], start=True, stop=True)
         nc.tensor.matmul(out=bias_narrow[:], lhsT=probs_t[:], rhs=bo_rows[:, NARROW], start=True, stop=True)
+        turn_a(1)
         project_wide(0)
         project_narrow(0)
-        turn_a(1)
         nc.scalar.copy(out=fused[:, WIDE], in_=bias_wide[:])
         nc.scalar.copy(out=fused[:, NARROW], in_=bias_narrow[:])
         regroup_a(1)
@@ -295,14 +295,15 @@ def tile_model_pa_kernel(tc, attn_ctx, Wo, bo, cluster_probs, out):
             project_wide(c - 1)
             project_narrow(c - 1)
 
-        quantise_w_narrow(C - 1)
-        project_narrow(C - 1)
-        mix_both(C - 2)
+        quantise_w(C - 1, "narrow")
+        project(C - 1, "narrow")
+        mix(C - 2, "wide")
         quantise_w(C - 1, "first")
         project(C - 1, "first")
-        mix(C - 1, "narrow")
+        mix(C - 2, "narrow")
         quantise_w(C - 1, "second")
         project(C - 1, "second")
+        mix(C - 1, "narrow")
         mix(C - 1, "first")
         mix(C - 1, "second")
 

from contextlib import ExitStack

import concourse.masks as masks
import concourse.mybir as mybir

BF16 = mybir.dt.bfloat16
F32 = mybir.dt.float32
U32 = mybir.dt.uint32
U8 = mybir.dt.uint8
FP8X4 = mybir.dt.float8_e4m3fn_x4
MULT = mybir.AluOpType.mult
ADD = mybir.AluOpType.add

P = 128
PACK = 4
HALVES = 2
B, C, L, G, E = 2, 16, 64, 512, 768
TOKENS = B * L
PAIRS = C // 2
assert TOKENS == P and G == P * PACK

N_WIDE = 512
N_NARROW = E - N_WIDE
WIDE = slice(0, N_WIDE)
NARROW = slice(N_WIDE, E)
FIRST = slice(0, N_NARROW)
SECOND = slice(N_NARROW, N_WIDE)
COLUMNS = {"wide": WIDE, "narrow": NARROW, "first": FIRST, "second": SECOND}
SIZE = {N_WIDE: "wide", N_NARROW: "narrow"}
BANKS = {"wide": "wide", "narrow": "narrow", "first": "wide", "second": "narrow"}
N_GPSIMD = 160
N_VECTOR_ODD = 128
N_VECTOR_EVEN = 112
VECTOR_AT_THE_ENDS = {0: 528, 1: 480, 2: 400, C - 1: 0}
VECTOR_SHARE = {c: VECTOR_AT_THE_ENDS.get(c, N_VECTOR_ODD if c % 2 == 1 else N_VECTOR_EVEN) for c in range(C)}
GPSIMD_SHARE = {0: 0, 1: 0}
N_TENSOR = 64
RUN = 8
RUN_SCALAR = 8
RUN_GPSIMD = 4

FLOPS = 2 * TOKENS * C * G * E


def tile_model_pa_kernel(tc, attn_ctx, Wo, bo, cluster_probs, out):
    nc = tc.nc
    with ExitStack() as ctx:
        consts = ctx.enter_context(tc.tile_pool(name="consts", bufs=1))
        a_in = ctx.enter_context(tc.tile_pool(name="a_in", bufs=PAIRS))
        w_in = ctx.enter_context(tc.tile_pool(name="w_in", bufs=C))
        work = ctx.enter_context(tc.tile_pool(name="work", bufs=3))
        psum = ctx.enter_context(tc.psum_pool(name="psum", bufs=2))
        ctx.enter_context(tc.manual_schedule())

        probs_bf16 = consts.tile([P, P], BF16)
        nc.vector.memset(probs_bf16[:, C:], 0.0)
        bo_rows = consts.tile([P, E], BF16)
        nc.vector.memset(bo_rows[:], 0.0)
        a_rows = attn_ctx.rearrange("b c l h d -> b (c l) (h d)")
        a_raw = []
        w_raw = []
        def load_a(pair):
            a_tile = a_in.tile([P, B * G], BF16, name="a_raw")
            nc.sync.dma_start(
                out=a_tile[:].rearrange("r (b k) -> r b k", b=B),
                in_=a_rows[:, pair * P : (pair + 1) * P, :].rearrange("b r k -> r b k"),
            )
            a_raw.append(a_tile)

        def load_w(c):
            w_tile = w_in.tile([P, PACK, E], BF16, name="w_raw")
            nc.sync.dma_start(
                out=w_tile[:],
                in_=Wo[c].rearrange("h d e -> (h d) e").rearrange("(p t) e -> p t e", t=PACK),
            )
            w_raw.append(w_tile)

        load_w(0)
        load_a(0)
        nc.sync.dma_start(out=probs_bf16[:, 0:C], in_=cluster_probs.rearrange("b l c -> (b l) c"))
        nc.sync.dma_start(out=bo_rows[0:C, :], in_=bo[:, :])
        load_w(1)
        for pair in range(1, PAIRS):
            load_a(pair)
            load_w(2 * pair)
            load_w(2 * pair + 1)

        identity = consts.tile([P, P], F32)
        masks.make_identity(nc, identity[:])
        identity_bf16 = consts.tile([P, P], BF16)
        masks.make_identity(nc, identity_bf16[:])
        probs = consts.tile([P, C], F32)

        a_codes = {}
        a_turned = {}
        a_grouped = {}
        w_grouped = {}
        w_routed = {}
        w_codes = {}
        projected = {}
        fused = consts.tile([P, E], F32)

        def turn_a(pair):
            words = a_raw[pair][:].bitcast(F32).rearrange("r (b p u) -> r b u p", b=B, u=HALVES)
            turned = psum.tile([P, B, HALVES, 2, L], F32, name="a_turned")
            for b in range(B):
                for u in range(HALVES):
                    nc.tensor.transpose(
                        turned[:, b, u, :, :].rearrange("p c l -> p (c l)"), words[:, b, u, :], identity[:]
                    )
            a_turned[pair] = turned

        def regroup_a(pair):
            turned = a_turned[pair]
            grouped = work.tile([P, 2 * TOKENS * PACK], BF16, name="a_grouped", align_bytes=64)
            grouped_words = grouped[:].bitcast(F32)
            nc.scalar.copy(
                out=grouped_words.rearrange("p (c b l u) -> p b c l u", c=2, b=B, u=HALVES),
                in_=turned[:].rearrange("p b u c l -> p b c l u"),
            )
            a_grouped[pair] = grouped

        def quantise_a(pair):
            codes = work.tile([P, 2 * TOKENS], U32, name="a_codes", align_bytes=64)
            scales = work.tile([P, 2 * TOKENS], U8, name="a_scales", align_bytes=64)
            nc.vector.quantize_mx(out=codes[:].bitcast(FP8X4), scales=scales[:], in_=a_grouped[pair][:])
            a_codes[pair] = (codes, scales)

        def regroup(copy, grouped, raw_columns, run=RUN):
            copy(
                out=grouped.rearrange("p (n i) t -> p n t i", i=run),
                in_=raw_columns.rearrange("p t (n i) -> p n t i", i=run),
            )

        def gpsimd_regroups_w(c):
            grouped = work.tile([P, E, PACK], BF16, name="w_grouped", bufs=2, align_bytes=64)
            w_grouped[c] = grouped
            columns = slice(E - GPSIMD_SHARE.get(c, N_GPSIMD), E)
            if columns.start < E:
                nc.gpsimd.tensor_scalar(
                    out=grouped[:, columns, :].rearrange("p (n i) t -> p n t i", i=RUN_GPSIMD),
                    in0=w_raw[c][:, :, columns].rearrange("p t (n i) -> p n t i", i=RUN_GPSIMD),
                    scalar1=1.0,
                    scalar2=0.0,
                    op0=MULT,
                    op1=ADD,
                )

        def vector_regroups_w(c):
            stop = E - GPSIMD_SHARE.get(c, N_GPSIMD)
            columns = slice(stop - VECTOR_SHARE[c], stop)
            if columns.start < stop:
                regroup(nc.vector.tensor_copy, w_grouped[c][:, columns, :], w_raw[c][:, :, columns])

        def tensor_regroups_w(c):
            stop = E - GPSIMD_SHARE.get(c, N_GPSIMD) - VECTOR_SHARE[c]
            routed = psum.tile([P, N_TENSOR, PACK], BF16, name="routed")
            nc.tensor.matmul(
                out=routed[:],
                lhsT=identity_bf16[:],
                rhs=w_raw[c][:, :, stop - N_TENSOR : stop].rearrange("p t n -> p n t"),
                start=True,
                stop=True,
            )
            w_routed[c] = routed

        def scalar_takes_routed(c):
            stop = E - GPSIMD_SHARE.get(c, N_GPSIMD) - VECTOR_SHARE[c]
            nc.scalar.copy(
                out=w_grouped[c][:, stop - N_TENSOR : stop, :].rearrange("p n t -> p (n t)").bitcast(F32),
                in_=w_routed[c][:].rearrange("p n t -> p (n t)").bitcast(F32),
            )

        def scalar_regroups_w(c):
            stop = E - GPSIMD_SHARE.get(c, N_GPSIMD) - VECTOR_SHARE[c] - N_TENSOR
            for columns in (slice(N_WIDE, stop), FIRST, SECOND) if c == C - 1 else (slice(0, stop),):
                regroup(nc.scalar.copy, w_grouped[c][:, columns, :], w_raw[c][:, :, columns], run=RUN_SCALAR)
                if columns.stop == stop:
                    scalar_takes_routed(c)

        def quantise_w(c, part):
            columns = COLUMNS[part]
            width = columns.stop - columns.start
            codes = work.tile([P, width], U32, name="w_codes_" + SIZE[width], align_bytes=64)
            scales = work.tile([P, width], U8, name="w_scales_" + SIZE[width], align_bytes=64)
            nc.vector.quantize_mx(
                out=codes[:].bitcast(FP8X4),
                scales=scales[:],
                in_=w_grouped[c][:, columns, :].rearrange("p n t -> p (n t)"),
            )
            w_codes[c, part] = (codes, scales)

        def quantise_w_wide(c):
            quantise_w(c, "wide")

        def quantise_w_narrow(c):
            quantise_w(c, "narrow")

        def project(c, part):
            tokens_codes, tokens_scales = a_codes[c // 2]
            tokens = slice((c % 2) * TOKENS, (c % 2 + 1) * TOKENS)
            codes, scales = w_codes[c, part]
            width = COLUMNS[part].stop - COLUMNS[part].start
            out_tile = psum.tile([P, width], F32, name="projected_" + BANKS[part])
            nc.tensor.matmul_mx(
                out=out_tile[:],
                lhsT=tokens_codes[:, tokens].bitcast(FP8X4),
                lhsT_scale=tokens_scales[:, tokens],
                rhs=codes[:].bitcast(FP8X4),
                rhs_scale=scales[:],
                start=True,
                stop=True,
            )
            projected[c, part] = out_tile

        def mix(c, part):
            columns = COLUMNS[part]
            nc.vector.scalar_tensor_tensor(
                out=fused[:, columns],
                in0=projected[c, part][:],
                scalar=probs[:, c : c + 1],
                in1=fused[:, columns],
                op0=MULT,
                op1=ADD,
            )

        def project_narrow(c):
            project(c, "narrow")

        def project_wide(c):
            project(c, "wide")

        def mix_both(c):
            mix(c, "wide")
            mix(c, "narrow")

        gpsimd_regroups_w(0)
        vector_regroups_w(0)
        tensor_regroups_w(0)
        scalar_regroups_w(0)
        turn_a(0)
        nc.vector.tensor_copy(out=probs[:], in_=probs_bf16[:, 0:C])
        probs_turned = psum.tile([P, P], BF16, name="routed")
        nc.tensor.transpose(probs_turned[:], probs_bf16[:], identity_bf16[:])
        regroup_a(0)
        probs_t = consts.tile([P, P], BF16)
        nc.scalar.copy(out=probs_t[:], in_=probs_turned[:])

        quantise_w_wide(0)
        quantise_w_narrow(0)
        quantise_a(0)
        gpsimd_regroups_w(1)
        vector_regroups_w(1)
        tensor_regroups_w(1)
        scalar_regroups_w(1)
        bias_wide = psum.tile([P, N_WIDE], F32, name="projected_wide")
        bias_narrow = psum.tile([P, N_NARROW], F32, name="projected_narrow")
        nc.tensor.matmul(out=bias_wide[:], lhsT=probs_t[:], rhs=bo_rows[:, WIDE], start=True, stop=True)
        nc.tensor.matmul(out=bias_narrow[:], lhsT=probs_t[:], rhs=bo_rows[:, NARROW], start=True, stop=True)
        turn_a(1)
        project_wide(0)
        project_narrow(0)
        nc.scalar.copy(out=fused[:, WIDE], in_=bias_wide[:])
        nc.scalar.copy(out=fused[:, NARROW], in_=bias_narrow[:])
        regroup_a(1)

        quantise_w_wide(1)
        quantise_w_narrow(1)
        gpsimd_regroups_w(2)
        vector_regroups_w(2)
        quantise_a(1)
        gpsimd_regroups_w(3)
        mix_both(0)
        tensor_regroups_w(2)
        scalar_regroups_w(2)
        project_wide(1)
        project_narrow(1)

        for c in range(3, C):
            next_pair_starts = c % 2 == 1 and c + 1 < C
            if next_pair_starts:
                turn_a((c + 1) // 2)
            tensor_regroups_w(c)
            quantise_w_wide(c - 1)
            quantise_w_narrow(c - 1)
            if c + 1 < C:
                gpsimd_regroups_w(c + 1)
            vector_regroups_w(c)
            if c % 2 == 0:
                quantise_a(c // 2)
            mix_both(c - 2)
            scalar_regroups_w(c)
            if next_pair_starts:
                regroup_a((c + 1) // 2)
            project_wide(c - 1)
            project_narrow(c - 1)

        quantise_w(C - 1, "narrow")
        project(C - 1, "narrow")
        mix(C - 2, "wide")
        quantise_w(C - 1, "first")
        project(C - 1, "first")
        mix(C - 2, "narrow")
        quantise_w(C - 1, "second")
        project(C - 1, "second")
        mix(C - 1, "narrow")
        mix(C - 1, "first")
        mix(C - 1, "second")

        out_rows = out.rearrange("b l e -> (b l) e")
        for columns in (NARROW, FIRST, SECOND):
            nc.sync.dma_start(out=out_rows[:, columns], in_=fused[:, columns])
